import numpy as np
import ml_dtypes


def mxq(x, axis, fmt="e4m3"):
    dtype, down = {"e4m3": (ml_dtypes.float8_e4m3fn, 7), "e5m2": (ml_dtypes.float8_e5m2, 14)}[fmt]
    v = np.moveaxis(np.asarray(x, np.float32).astype(ml_dtypes.bfloat16).astype(np.float64), axis, -1)
    blocks = v.reshape(v.shape[:-1] + (-1, 32))
    amax = np.abs(blocks).max(-1, keepdims=True)
    byte = np.maximum(np.where(amax > 0, np.frexp(amax)[1] - 1 + 127, 0) - down, 1)
    scale = np.exp2(byte - 127.0)
    codes = (blocks / scale).astype(np.float32).astype(dtype).astype(np.float64)
    return np.moveaxis((codes * scale).reshape(v.shape), -1, axis)


WIDE = False


def mx_kscale(k):
    if not WIDE:
        return np.ones(k)
    levels = np.array([20, -20, 10, -10, 0])
    a = np.random.permutation(np.resize(levels, k // 512 * 4)).reshape(k // 512, 4)
    idx = np.arange(k)
    return np.exp2(a[idx // 512, idx % 128 // 32])


BF16 = ml_dtypes.bfloat16


def bf(x):
    return np.asarray(x, np.float32).astype(BF16)


def f64(x):
    return np.asarray(x).astype(np.float64)


B, P, L, FI, FO = 16, 2, 3, 256, 512
C = (L + 1) * (L + 1)


def setup_inputs():
    u = mx_kscale(FO)
    x = np.random.standard_normal((B, P, C, FI))
    W_e = np.random.standard_normal((L + 1, FI, FO)) / np.sqrt(FI) / u
    W_o = np.random.standard_normal((L + 1, FI, FO)) / np.sqrt(FI) / u
    b = np.random.standard_normal(FO) * 0.5
    g = np.random.standard_normal((B, P, C, FO)) * np.exp2(np.random.randint(-12, 1, (B, P, C, 1))) * 16.0 * u
    return {"x": bf(x), "W_e": bf(W_e), "W_o": bf(W_o), "b": bf(b), "grad_out": bf(g)}


def reference(x, W_e, W_o, b, grad_out):
    gq = mxq(f64(grad_out), 3, "e5m2")
    weq = mxq(f64(W_e), 2, "e4m3")
    woq = mxq(f64(W_o), 2, "e4m3")
    gs_e, gs_o = [], []
    for l in range(L + 1):
        seg = gq[:, :, l * l:(l + 1) * (l + 1), :]
        gs_e.append(seg[:, 0] @ weq[l].T)
        gs_o.append(seg[:, 1] @ woq[l].T)
    return np.stack([np.concatenate(gs_e, axis=-2), np.concatenate(gs_o, axis=-2)], axis=-3)

@@ -1,0 +1,139 @@
+from contextlib import ExitStack
+
+import concourse.mybir as mybir
+from concourse.masks import make_identity
+
+F32 = mybir.dt.float32
+BF16 = mybir.dt.bfloat16
+U32 = mybir.dt.uint32
+U8 = mybir.dt.uint8
+E4M3X4 = mybir.dt.float8_e4m3fn_x4
+E5M2X4 = mybir.dt.float8_e5m2_x4
+
+P = 128
+ITEMS = 16
+PARITIES = 2
+COMPONENTS = 16
+FI = 256
+FO = 512
+WORDS = FO // 2
+ROWS = ITEMS * PARITIES * COMPONENTS
+ROW_BLOCKS = ROWS // P
+
+DEGREE_PAIRS = ((3, 0), (2, 1))
+
+FLOPS = 2 * ROWS * FO * FI
+BYTES = 2 * (2 * 4 * FI * FO) + 2 * ROWS * FO + 4 * ROWS * FI
+
+
+def width(degree):
+    return 2 * degree + 1
+
+
+def first_component(degree):
+    return degree * degree
+
+
+def tile_dense_pa_s_kernel(tc, x, W_e, W_o, b, grad_out, out):
+    nc = tc.nc
+    weights = (W_e, W_o)
+    with ExitStack() as ctx:
+        keep = ctx.enter_context(tc.tile_pool(name="keep", bufs=1))
+        flipped = ctx.enter_context(tc.psum_pool(name="flipped", bufs=6))
+        sums = ctx.enter_context(tc.psum_pool(name="sums", bufs=2))
+
+        g_raw = keep.tile([P, ROW_BLOCKS, FO], BF16, name="g_raw")
+        g_rows = grad_out.rearrange("n s c k -> (n s c) k").rearrange("(t p) k -> p t k", p=P)
+        for half in range(2):
+            nc.sync.dma_start(out=g_raw[:, 2 * half : 2 * half + 2, :], in_=g_rows[:, 2 * half : 2 * half + 2, :])
+
+        w_raw = {}
+        for parity in range(PARITIES):
+            for pair in DEGREE_PAIRS:
+                for degree in pair:
+                    w_raw[parity, degree] = keep.tile([P, 2 * FO], BF16, name="w_raw_%d_%d" % (parity, degree))
+                    nc.sync.dma_start(
+                        out=w_raw[parity, degree][:],
+                        in_=weights[parity][degree].rearrange("(p h) k -> p (h k)", h=2),
+                    )
+
+        ident = keep.tile([P, P], F32, name="ident")
+        make_identity(nc, ident[:])
+
+        g_grouped = keep.tile([P, 4 * ROWS], BF16, name="g_grouped", align_bytes=64)
+        g_codes = keep.tile([P, ROWS], U32, name="g_codes", align_bytes=64)
+        g_scales = keep.tile([P, ROWS], U8, name="g_scales", align_bytes=64)
+        g_words = g_grouped[:].bitcast(F32).rearrange("q (g r u) -> q g r u", r=P, u=2)
+        for half in range(2):
+            g_flip = flipped.tile([P, 2, 2 * P], F32, name="g_flip", tag="flip")
+            for t in range(2):
+                for u in range(2):
+                    nc.tensor.transpose(
+                        g_flip[:, u, P * t : P * t + P],
+                        g_raw[:, 2 * half + t, :].bitcast(F32)[:, P * u : P * u + P],
+                        ident[:],
+                    )
+            by_row = g_flip[:].rearrange("q u (n s c) -> q u n s c", s=PARITIES, c=COMPONENTS)
+            items = ITEMS // 2
+            for parity in range(PARITIES):
+                for pair_index, pair in enumerate(DEGREE_PAIRS):
+                    start = 0
+                    for degree in pair:
+                        w = width(degree)
+                        c0 = first_component(degree)
+                        src = by_row[:, :, :, parity, c0 : c0 + w].rearrange("q u n w -> q n w u")
+                        r0 = start + half * items * w
+                        dst = g_words[:, 2 * parity + pair_index, r0 : r0 + items * w, :].rearrange(
+                            "q (n w) u -> q n w u", w=w
+                        )
+                        if half == 0:
+                            nc.vector.tensor_copy(out=dst, in_=src)
+                        else:
+                            nc.scalar.copy(out=dst, in_=src)
+                        start += ITEMS * w
+        nc.vector.quantize_mx(out=g_codes[:].bitcast(E5M2X4), scales=g_scales[:], in_=g_grouped[:])
+
+        for parity in range(PARITIES):
+            for pair_index, pair in enumerate(DEGREE_PAIRS):
+                group = 2 * parity + pair_index
+                w_grouped = keep.tile([P, 2, 4 * FI], BF16, name="w_grouped_%d" % group, align_bytes=64)
+                w_codes = keep.tile([P, 2, FI], U32, name="w_codes_%d" % group, align_bytes=64)
+                w_scales = keep.tile([P, 2, FI], U8, name="w_scales_%d" % group, align_bytes=64)
+                for side, degree in enumerate(pair):
+                    w_flip = flipped.tile([P, 4, P], F32, name="w_flip", tag="flip")
+                    for a in range(4):
+                        nc.tensor.transpose(
+                            w_flip[:, a, :],
+                            w_raw[parity, degree][:].bitcast(F32)[:, P * a : P * a + P],
+                            ident[:],
+                        )
+                    nc.scalar.copy(
+                        out=w_grouped[:, side, :].bitcast(F32).rearrange("q (p a) -> q p a", a=4),
+                        in_=w_flip[:].rearrange("q a p -> q p a"),
+                    )
+                    nc.vector.quantize_mx(
+                        out=w_codes[:, side, :].bitcast(E4M3X4),
+                        scales=w_scales[:, side, :],
+                        in_=w_grouped[:, side, :],
+                    )
+                acc = sums.tile([P, 2 * FI], F32, name="acc")
+                nc.tensor.matmul_mx(
+                    out=acc[:],
+                    lhsT=g_codes[:, P * group : P * group + P].bitcast(E5M2X4),
+                    lhsT_scale=g_scales[:, P * group : P * group + P],
+                    rhs=w_codes[:].rearrange("q s f -> q (s f)").bitcast(E4M3X4),
+                    rhs_scale=w_scales[:].rearrange("q s f -> q (s f)"),
+                    start=True,
+                    stop=True,
+                )
+                result = keep.tile([P, 2 * FI], F32, name="result_%d" % group)
+                nc.vector.tensor_copy(out=result[:], in_=acc[:])
+                start = 0
+                for side, degree in enumerate(pair):
+                    w = width(degree)
+                    c0 = first_component(degree)
+                    nc.sync.dma_start(
+                        out=out[:, parity, c0 : c0 + w, :],
+                        in_=result[start : start + ITEMS * w, FI * side : FI * side + FI],
+                    )
+                    start += ITEMS * w

@@ -16,11 +16,11 @@ PARITIES = 2
 COMPONENTS = 16
 FI = 256
 FO = 512
-WORDS = FO // 2
 ROWS = ITEMS * PARITIES * COMPONENTS
 ROW_BLOCKS = ROWS // P
 
-DEGREE_PAIRS = ((3, 0), (2, 1))
+DEGREE_PAIRS = ((2, 1), (3, 0))
+GROUPS = tuple((parity, pair) for parity in range(PARITIES) for pair in DEGREE_PAIRS)
 
 FLOPS = 2 * ROWS * FO * FI
 BYTES = 2 * (2 * 4 * FI * FO) + 2 * ROWS * FO + 4 * ROWS * FI
@@ -38,24 +38,24 @@ def tile_dense_pa_s_kernel(tc, x, W_e, W_o, b, grad_out, out):
     nc = tc.nc
     weights = (W_e, W_o)
     with ExitStack() as ctx:
+        ctx.enter_context(tc.manual_schedule())
         keep = ctx.enter_context(tc.tile_pool(name="keep", bufs=1))
         flipped = ctx.enter_context(tc.psum_pool(name="flipped", bufs=6))
         sums = ctx.enter_context(tc.psum_pool(name="sums", bufs=2))
 
         g_raw = keep.tile([P, ROW_BLOCKS, FO], BF16, name="g_raw")
         g_rows = grad_out.rearrange("n s c k -> (n s c) k").rearrange("(t p) k -> p t k", p=P)
-        for half in range(2):
-            nc.sync.dma_start(out=g_raw[:, 2 * half : 2 * half + 2, :], in_=g_rows[:, 2 * half : 2 * half + 2, :])
+        for t in range(ROW_BLOCKS):
+            nc.sync.dma_start(out=g_raw[:, t, :], in_=g_rows[:, t, :])
 
         w_raw = {}
-        for parity in range(PARITIES):
-            for pair in DEGREE_PAIRS:
-                for degree in pair:
-                    w_raw[parity, degree] = keep.tile([P, 2 * FO], BF16, name="w_raw_%d_%d" % (parity, degree))
-                    nc.sync.dma_start(
-                        out=w_raw[parity, degree][:],
-                        in_=weights[parity][degree].rearrange("(p h) k -> p (h k)", h=2),
-                    )
+        for parity, pair in GROUPS:
+            for degree in pair:
+                w_raw[parity, degree] = keep.tile([P, 2 * FO], BF16, name="w_raw_%d_%d" % (parity, degree))
+                nc.sync.dma_start(
+                    out=w_raw[parity, degree][:],
+                    in_=weights[parity][degree].rearrange("(p h) k -> p (h k)", h=2),
+                )
 
         ident = keep.tile([P, P], F32, name="ident")
         make_identity(nc, ident[:])
@@ -64,6 +64,7 @@ def tile_dense_pa_s_kernel(tc, x, W_e, W_o, b, grad_out, out):
         g_codes = keep.tile([P, ROWS], U32, name="g_codes", align_bytes=64)
         g_scales = keep.tile([P, ROWS], U8, name="g_scales", align_bytes=64)
         g_words = g_grouped[:].bitcast(F32).rearrange("q (g r u) -> q g r u", r=P, u=2)
+        items = ITEMS // 2
         for half in range(2):
             g_flip = flipped.tile([P, 2, 2 * P], F32, name="g_flip", tag="flip")
             for t in range(2):
@@ -74,66 +75,73 @@ def tile_dense_pa_s_kernel(tc, x, W_e, W_o, b, grad_out, out):
                         ident[:],
                     )
             by_row = g_flip[:].rearrange("q u (n s c) -> q u n s c", s=PARITIES, c=COMPONENTS)
-            items = ITEMS // 2
-            for parity in range(PARITIES):
-                for pair_index, pair in enumerate(DEGREE_PAIRS):
-                    start = 0
-                    for degree in pair:
-                        w = width(degree)
-                        c0 = first_component(degree)
-                        src = by_row[:, :, :, parity, c0 : c0 + w].rearrange("q u n w -> q n w u")
-                        r0 = start + half * items * w
-                        dst = g_words[:, 2 * parity + pair_index, r0 : r0 + items * w, :].rearrange(
-                            "q (n w) u -> q n w u", w=w
-                        )
-                        if half == 0:
-                            nc.vector.tensor_copy(out=dst, in_=src)
-                        else:
-                            nc.scalar.copy(out=dst, in_=src)
-                        start += ITEMS * w
-        nc.vector.quantize_mx(out=g_codes[:].bitcast(E5M2X4), scales=g_scales[:], in_=g_grouped[:])
-
-        for parity in range(PARITIES):
-            for pair_index, pair in enumerate(DEGREE_PAIRS):
-                group = 2 * parity + pair_index
-                w_grouped = keep.tile([P, 2, 4 * FI], BF16, name="w_grouped_%d" % group, align_bytes=64)
-                w_codes = keep.tile([P, 2, FI], U32, name="w_codes_%d" % group, align_bytes=64)
-                w_scales = keep.tile([P, 2, FI], U8, name="w_scales_%d" % group, align_bytes=64)
-                for side, degree in enumerate(pair):
-                    w_flip = flipped.tile([P, 4, P], F32, name="w_flip", tag="flip")
-                    for a in range(4):
-                        nc.tensor.transpose(
-                            w_flip[:, a, :],
-                            w_raw[parity, degree][:].bitcast(F32)[:, P * a : P * a + P],
-                            ident[:],
-                        )
-                    nc.scalar.copy(
-                        out=w_grouped[:, side, :].bitcast(F32).rearrange("q (p a) -> q p a", a=4),
-                        in_=w_flip[:].rearrange("q a p -> q p a"),
-                    )
-                    nc.vector.quantize_mx(
-                        out=w_codes[:, side, :].bitcast(E4M3X4),
-                        scales=w_scales[:, side, :],
-                        in_=w_grouped[:, side, :],
-                    )
-                acc = sums.tile([P, 2 * FI], F32, name="acc")
-                nc.tensor.matmul_mx(
-                    out=acc[:],
-                    lhsT=g_codes[:, P * group : P * group + P].bitcast(E5M2X4),
-                    lhsT_scale=g_scales[:, P * group : P * group + P],
-                    rhs=w_codes[:].rearrange("q s f -> q (s f)").bitcast(E4M3X4),
-                    rhs_scale=w_scales[:].rearrange("q s f -> q (s f)"),
-                    start=True,
-                    stop=True,
-                )
-                result = keep.tile([P, 2 * FI], F32, name="result_%d" % group)
-                nc.vector.tensor_copy(out=result[:], in_=acc[:])
+            for group, (parity, pair) in enumerate(GROUPS):
                 start = 0
-                for side, degree in enumerate(pair):
+                for degree in pair:
                     w = width(degree)
                     c0 = first_component(degree)
-                    nc.sync.dma_start(
-                        out=out[:, parity, c0 : c0 + w, :],
-                        in_=result[start : start + ITEMS * w, FI * side : FI * side + FI],
-                    )
+                    src = by_row[:, :, :, parity, c0 : c0 + w].rearrange("q u n w -> q n w u")
+                    r0 = start + half * items * w
+                    dst = g_words[:, group, r0 : r0 + items * w, :].rearrange("q (n w) u -> q n w u", w=w)
+                    if half == 0:
+                        nc.vector.tensor_copy(out=dst, in_=src)
+                    else:
+                        nc.scalar.copy(out=dst, in_=src)
                     start += ITEMS * w
+        nc.vector.quantize_mx(out=g_codes[:].bitcast(E5M2X4), scales=g_scales[:], in_=g_grouped[:])
+
+        w_codes = {}
+        w_scales = {}
+
+        def quantise_weights(group):
+            parity, pair = GROUPS[group]
+            w_grouped = keep.tile([P, 2, 4 * FI], BF16, name="w_grouped_%d" % group, align_bytes=64)
+            w_codes[group] = keep.tile([P, 2, FI], U32, name="w_codes_%d" % group, align_bytes=64)
+            w_scales[group] = keep.tile([P, 2, FI], U8, name="w_scales_%d" % group, align_bytes=64)
+            for side, degree in enumerate(pair):
+                w_flip = flipped.tile([P, 4, P], F32, name="w_flip", tag="flip")
+                for a in range(4):
+                    nc.tensor.transpose(
+                        w_flip[:, a, :],
+                        w_raw[parity, degree][:].bitcast(F32)[:, P * a : P * a + P],
+                        ident[:],
+                    )
+                nc.scalar.copy(
+                    out=w_grouped[:, side, :].bitcast(F32).rearrange("q (p a) -> q p a", a=4),
+                    in_=w_flip[:].rearrange("q a p -> q p a"),
+                )
+                nc.vector.quantize_mx(
+                    out=w_codes[group][:, side, :].bitcast(E4M3X4),
+                    scales=w_scales[group][:, side, :],
+                    in_=w_grouped[:, side, :],
+                )
+
+        def multiply(group):
+            parity, pair = GROUPS[group]
+            acc = sums.tile([P, 2 * FI], F32, name="acc")
+            nc.tensor.matmul_mx(
+                out=acc[:],
+                lhsT=g_codes[:, P * group : P * group + P].bitcast(E5M2X4),
+                lhsT_scale=g_scales[:, P * group : P * group + P],
+                rhs=w_codes[group][:].rearrange("q s f -> q (s f)").bitcast(E4M3X4),
+                rhs_scale=w_scales[group][:].rearrange("q s f -> q (s f)"),
+                start=True,
+                stop=True,
+            )
+            result = keep.tile([P, 2 * FI], F32, name="result_%d" % group)
+            nc.vector.tensor_copy(out=result[:], in_=acc[:])
+            for side in (1, 0):
+                degree = pair[side]
+                w = width(degree)
+                c0 = first_component(degree)
+                start = side * ITEMS * width(pair[0])
+                nc.sync.dma_start(
+                    out=out[:, parity, c0 : c0 + w, :],
+                    in_=result[start : start + ITEMS * w, FI * side : FI * side + FI],
+                )
+
+        quantise_weights(0)
+        for group in range(len(GROUPS)):
+            if group + 1 < len(GROUPS):
+                quantise_weights(group + 1)
+            multiply(group)

@@ -7,6 +7,7 @@ F32 = mybir.dt.float32
 BF16 = mybir.dt.bfloat16
 U32 = mybir.dt.uint32
 U8 = mybir.dt.uint8
+I32 = mybir.dt.int32
 E4M3X4 = mybir.dt.float8_e4m3fn_x4
 E5M2X4 = mybir.dt.float8_e5m2_x4
 
@@ -21,6 +22,9 @@ ROW_BLOCKS = ROWS // P
 
 DEGREE_PAIRS = ((2, 1), (3, 0))
 GROUPS = tuple((parity, pair) for parity in range(PARITIES) for pair in DEGREE_PAIRS)
+
+IDLE_PASSES_AT_START = 3
+IDLE_PASSES_AFTER_TRANSPOSES = 2
 
 FLOPS = 2 * ROWS * FO * FI
 BYTES = 2 * (2 * 4 * FI * FO) + 2 * ROWS * FO + 4 * ROWS * FI
@@ -40,8 +44,9 @@ def tile_dense_pa_s_kernel(tc, x, W_e, W_o, b, grad_out, out):
     with ExitStack() as ctx:
         ctx.enter_context(tc.manual_schedule())
         keep = ctx.enter_context(tc.tile_pool(name="keep", bufs=1))
-        flipped = ctx.enter_context(tc.psum_pool(name="flipped", bufs=6))
+        flipped = ctx.enter_context(tc.psum_pool(name="flipped", bufs=5))
         sums = ctx.enter_context(tc.psum_pool(name="sums", bufs=2))
+        idle = ctx.enter_context(tc.psum_pool(name="idle", bufs=1))
 
         g_raw = keep.tile([P, ROW_BLOCKS, FO], BF16, name="g_raw")
         g_rows = grad_out.rearrange("n s c k -> (n s c) k").rearrange("(t p) k -> p t k", p=P)
@@ -59,6 +64,30 @@ def tile_dense_pa_s_kernel(tc, x, W_e, W_o, b, grad_out, out):
 
         ident = keep.tile([P, P], F32, name="ident")
         make_identity(nc, ident[:])
+
+        zeros = keep.tile([P, 8 * FI], BF16, name="zeros", align_bytes=64)
+        idle_rows = keep.tile([P, P], U32, name="idle_rows", align_bytes=64)
+        idle_rows_scales = keep.tile([P, P], U8, name="idle_rows_scales", align_bytes=64)
+        idle_weights = keep.tile([P, 2 * FI], U32, name="idle_weights", align_bytes=64)
+        idle_weights_scales = keep.tile([P, 2 * FI], U8, name="idle_weights_scales", align_bytes=64)
+        nc.vector.memset(zeros[:].bitcast(I32), 0)
+        nc.vector.quantize_mx(out=idle_weights[:].bitcast(E4M3X4), scales=idle_weights_scales[:], in_=zeros[:])
+        nc.vector.quantize_mx(out=idle_rows[:].bitcast(E5M2X4), scales=idle_rows_scales[:], in_=zeros[:, 0 : 4 * P])
+        idle_sums = idle.tile([P, 2 * FI], F32, name="idle_sums")
+
+        def keep_clock_up(passes):
+            for i in range(passes):
+                nc.tensor.matmul_mx(
+                    out=idle_sums[:],
+                    lhsT=idle_rows[:].bitcast(E5M2X4),
+                    lhsT_scale=idle_rows_scales[:],
+                    rhs=idle_weights[:].bitcast(E4M3X4),
+                    rhs_scale=idle_weights_scales[:],
+                    start=True,
+                    stop=True,
+                )
+
+        keep_clock_up(IDLE_PASSES_AT_START)
 
         g_grouped = keep.tile([P, 4 * ROWS], BF16, name="g_grouped", align_bytes=64)
         g_codes = keep.tile([P, ROWS], U32, name="g_codes", align_bytes=64)
@@ -88,6 +117,7 @@ def tile_dense_pa_s_kernel(tc, x, W_e, W_o, b, grad_out, out):
                     else:
                         nc.scalar.copy(out=dst, in_=src)
                     start += ITEMS * w
+        keep_clock_up(IDLE_PASSES_AFTER_TRANSPOSES)
         nc.vector.quantize_mx(out=g_codes[:].bitcast(E5M2X4), scales=g_scales[:], in_=g_grouped[:])
 
         w_codes = {}
@@ -141,6 +171,7 @@ def tile_dense_pa_s_kernel(tc, x, W_e, W_o, b, grad_out, out):
                 )
 
         quantise_weights(0)
+        keep_clock_up(IDLE_PASSES_AFTER_TRANSPOSES)
         for group in range(len(GROUPS)):
             if group + 1 < len(GROUPS):
                 quantise_weights(group + 1)

@@ -7,7 +7,6 @@ F32 = mybir.dt.float32
 BF16 = mybir.dt.bfloat16
 U32 = mybir.dt.uint32
 U8 = mybir.dt.uint8
-I32 = mybir.dt.int32
 E4M3X4 = mybir.dt.float8_e4m3fn_x4
 E5M2X4 = mybir.dt.float8_e5m2_x4
 
@@ -23,19 +22,30 @@ ROW_BLOCKS = ROWS // P
 DEGREE_PAIRS = ((2, 1), (3, 0))
 GROUPS = tuple((parity, pair) for parity in range(PARITIES) for pair in DEGREE_PAIRS)
 
-IDLE_PASSES_AT_START = 3
-IDLE_PASSES_AFTER_TRANSPOSES = 2
+LOOKAHEAD = 2
 
 FLOPS = 2 * ROWS * FO * FI
 BYTES = 2 * (2 * 4 * FI * FO) + 2 * ROWS * FO + 4 * ROWS * FI
 
 
-def width(degree):
-    return 2 * degree + 1
+def component_blocks(degree):
+    blocks = []
+    c0 = degree * degree
+    for w in (4, 2, 1):
+        if (2 * degree + 1) & w:
+            blocks.append((c0, w))
+            c0 += w
+    return blocks
 
 
-def first_component(degree):
-    return degree * degree
+def group_layout(pair):
+    layout = []
+    r0 = 0
+    for side, degree in enumerate(pair):
+        for c0, w in component_blocks(degree):
+            layout.append((side, c0, w, r0))
+            r0 += ITEMS * w
+    return layout
 
 
 def tile_dense_pa_s_kernel(tc, x, W_e, W_o, b, grad_out, out):
@@ -44,9 +54,8 @@ def tile_dense_pa_s_kernel(tc, x, W_e, W_o, b, grad_out, out):
     with ExitStack() as ctx:
         ctx.enter_context(tc.manual_schedule())
         keep = ctx.enter_context(tc.tile_pool(name="keep", bufs=1))
-        flipped = ctx.enter_context(tc.psum_pool(name="flipped", bufs=5))
+        flipped = ctx.enter_context(tc.psum_pool(name="flipped", bufs=6))
         sums = ctx.enter_context(tc.psum_pool(name="sums", bufs=2))
-        idle = ctx.enter_context(tc.psum_pool(name="idle", bufs=1))
 
         g_raw = keep.tile([P, ROW_BLOCKS, FO], BF16, name="g_raw")
         g_rows = grad_out.rearrange("n s c k -> (n s c) k").rearrange("(t p) k -> p t k", p=P)
@@ -65,30 +74,6 @@ def tile_dense_pa_s_kernel(tc, x, W_e, W_o, b, grad_out, out):
         ident = keep.tile([P, P], F32, name="ident")
         make_identity(nc, ident[:])
 
-        zeros = keep.tile([P, 8 * FI], BF16, name="zeros", align_bytes=64)
-        idle_rows = keep.tile([P, P], U32, name="idle_rows", align_bytes=64)
-        idle_rows_scales = keep.tile([P, P], U8, name="idle_rows_scales", align_bytes=64)
-        idle_weights = keep.tile([P, 2 * FI], U32, name="idle_weights", align_bytes=64)
-        idle_weights_scales = keep.tile([P, 2 * FI], U8, name="idle_weights_scales", align_bytes=64)
-        nc.vector.memset(zeros[:].bitcast(I32), 0)
-        nc.vector.quantize_mx(out=idle_weights[:].bitcast(E4M3X4), scales=idle_weights_scales[:], in_=zeros[:])
-        nc.vector.quantize_mx(out=idle_rows[:].bitcast(E5M2X4), scales=idle_rows_scales[:], in_=zeros[:, 0 : 4 * P])
-        idle_sums = idle.tile([P, 2 * FI], F32, name="idle_sums")
-
-        def keep_clock_up(passes):
-            for i in range(passes):
-                nc.tensor.matmul_mx(
-                    out=idle_sums[:],
-                    lhsT=idle_rows[:].bitcast(E5M2X4),
-                    lhsT_scale=idle_rows_scales[:],
-                    rhs=idle_weights[:].bitcast(E4M3X4),
-                    rhs_scale=idle_weights_scales[:],
-                    start=True,
-                    stop=True,
-                )
-
-        keep_clock_up(IDLE_PASSES_AT_START)
-
         g_grouped = keep.tile([P, 4 * ROWS], BF16, name="g_grouped", align_bytes=64)
         g_codes = keep.tile([P, ROWS], U32, name="g_codes", align_bytes=64)
         g_scales = keep.tile([P, ROWS], U8, name="g_scales", align_bytes=64)
@@ -105,19 +90,14 @@ def tile_dense_pa_s_kernel(tc, x, W_e, W_o, b, grad_out, out):
                     )
             by_row = g_flip[:].rearrange("q u (n s c) -> q u n s c", s=PARITIES, c=COMPONENTS)
             for group, (parity, pair) in enumerate(GROUPS):
-                start = 0
-                for degree in pair:
-                    w = width(degree)
-                    c0 = first_component(degree)
+                for side, c0, w, r0 in group_layout(pair):
                     src = by_row[:, :, :, parity, c0 : c0 + w].rearrange("q u n w -> q n w u")
-                    r0 = start + half * items * w
-                    dst = g_words[:, group, r0 : r0 + items * w, :].rearrange("q (n w) u -> q n w u", w=w)
+                    r1 = r0 + half * items * w
+                    dst = g_words[:, group, r1 : r1 + items * w, :].rearrange("q (n w) u -> q n w u", w=w)
                     if half == 0:
                         nc.vector.tensor_copy(out=dst, in_=src)
                     else:
                         nc.scalar.copy(out=dst, in_=src)
-                    start += ITEMS * w
-        keep_clock_up(IDLE_PASSES_AFTER_TRANSPOSES)
         nc.vector.quantize_mx(out=g_codes[:].bitcast(E5M2X4), scales=g_scales[:], in_=g_grouped[:])
 
         w_codes = {}
@@ -148,9 +128,9 @@ def tile_dense_pa_s_kernel(tc, x, W_e, W_o, b, grad_out, out):
 
         def multiply(group):
             parity, pair = GROUPS[group]
-            acc = sums.tile([P, 2 * FI], F32, name="acc")
+            acc = sums.tile([P, 2, FI], F32, name="acc")
             nc.tensor.matmul_mx(
-                out=acc[:],
+                out=acc[:].rearrange("r s f -> r (s f)"),
                 lhsT=g_codes[:, P * group : P * group + P].bitcast(E5M2X4),
                 lhsT_scale=g_scales[:, P * group : P * group + P],
                 rhs=w_codes[group][:].rearrange("q s f -> q (s f)").bitcast(E4M3X4),
@@ -158,21 +138,22 @@ def tile_dense_pa_s_kernel(tc, x, W_e, W_o, b, grad_out, out):
                 start=True,
                 stop=True,
             )
-            result = keep.tile([P, 2 * FI], F32, name="result_%d" % group)
-            nc.vector.tensor_copy(out=result[:], in_=acc[:])
-            for side in (1, 0):
-                degree = pair[side]
-                w = width(degree)
-                c0 = first_component(degree)
-                start = side * ITEMS * width(pair[0])
-                nc.sync.dma_start(
-                    out=out[:, parity, c0 : c0 + w, :],
-                    in_=result[start : start + ITEMS * w, FI * side : FI * side + FI],
-                )
+            result = keep.tile([P, 2, FI], F32, name="result_%d" % group)
+            for side in range(2):
+                if group % 2 == 0:
+                    nc.vector.tensor_copy(out=result[:, side, :], in_=acc[:, side, :])
+                else:
+                    nc.scalar.copy(out=result[:, side, :], in_=acc[:, side, :])
+                for block_side, c0, w, r0 in group_layout(pair):
+                    if block_side == side:
+                        nc.sync.dma_start(
+                            out=out[:, parity, c0 : c0 + w, :],
+                            in_=result[r0 : r0 + ITEMS * w, side, :],
+                        )
 
-        quantise_weights(0)
-        keep_clock_up(IDLE_PASSES_AFTER_TRANSPOSES)
+        for group in range(LOOKAHEAD):
+            quantise_weights(group)
         for group in range(len(GROUPS)):
-            if group + 1 < len(GROUPS):
-                quantise_weights(group + 1)
+            if group + LOOKAHEAD < len(GROUPS):
+                quantise_weights(group + LOOKAHEAD)
             multiply(group)

@@ -9,43 +9,25 @@ U32 = mybir.dt.uint32
 U8 = mybir.dt.uint8
 E4M3X4 = mybir.dt.float8_e4m3fn_x4
 E5M2X4 = mybir.dt.float8_e5m2_x4
+COPY = mybir.ActivationFunctionType.Copy
+ADD = mybir.AluOpType.add
+MULT = mybir.AluOpType.mult
+AXES = mybir.AxisListType.XY
 
 P = 128
 ITEMS = 16
 PARITIES = 2
 COMPONENTS = 16
+DEGREES = 4
 FI = 256
 FO = 512
 ROWS = ITEMS * PARITIES * COMPONENTS
-ROW_BLOCKS = ROWS // P
 
-DEGREE_PAIRS = ((2, 1), (3, 0))
-GROUPS = tuple((parity, pair) for parity in range(PARITIES) for pair in DEGREE_PAIRS)
-
-LOOKAHEAD = 2
+HALF = COMPONENTS // 2
+LOW, HIGH = 0, 1
 
 FLOPS = 2 * ROWS * FO * FI
-BYTES = 2 * (2 * 4 * FI * FO) + 2 * ROWS * FO + 4 * ROWS * FI
-
-
-def component_blocks(degree):
-    blocks = []
-    c0 = degree * degree
-    for w in (4, 2, 1):
-        if (2 * degree + 1) & w:
-            blocks.append((c0, w))
-            c0 += w
-    return blocks
-
-
-def group_layout(pair):
-    layout = []
-    r0 = 0
-    for side, degree in enumerate(pair):
-        for c0, w in component_blocks(degree):
-            layout.append((side, c0, w, r0))
-            r0 += ITEMS * w
-    return layout
+BYTES = 2 * (2 * DEGREES * FI * FO) + 2 * ROWS * FO + 4 * ROWS * FI
 
 
 def tile_dense_pa_s_kernel(tc, x, W_e, W_o, b, grad_out, out):
@@ -54,106 +36,135 @@ def tile_dense_pa_s_kernel(tc, x, W_e, W_o, b, grad_out, out):
     with ExitStack() as ctx:
         ctx.enter_context(tc.manual_schedule())
         keep = ctx.enter_context(tc.tile_pool(name="keep", bufs=1))
-        flipped = ctx.enter_context(tc.psum_pool(name="flipped", bufs=6))
-        sums = ctx.enter_context(tc.psum_pool(name="sums", bufs=2))
+        flipped = ctx.enter_context(tc.psum_pool(name="flipped", bufs=5))
+        sums = ctx.enter_context(tc.psum_pool(name="sums", bufs=3))
 
-        g_raw = keep.tile([P, ROW_BLOCKS, FO], BF16, name="g_raw")
-        g_rows = grad_out.rearrange("n s c k -> (n s c) k").rearrange("(t p) k -> p t k", p=P)
-        for t in range(ROW_BLOCKS):
-            nc.sync.dma_start(out=g_raw[:, t, :], in_=g_rows[:, t, :])
+        pieces = []
+        for s in range(PARITIES):
+            pieces += [("g", s, HIGH), ("w", s, 3), ("w", s, 2), ("g", s, LOW), ("w", s, 1), ("w", s, 0)]
 
-        w_raw = {}
-        for parity, pair in GROUPS:
-            for degree in pair:
-                w_raw[parity, degree] = keep.tile([P, 2 * FO], BF16, name="w_raw_%d_%d" % (parity, degree))
+        raw = {}
+        for piece in pieces:
+            kind, s, i = piece
+            if kind == "g":
+                raw[piece] = keep.tile([P, FO], BF16, name="g_raw_%d_%d" % (s, i))
+                nc.sync.dma_start(out=raw[piece][:], in_=grad_out[:, s, HALF * i : HALF * i + HALF, :])
+            else:
+                raw[piece] = keep.tile([P, 2 * FO], BF16, name="w_raw_%d_%d" % (s, i))
                 nc.sync.dma_start(
-                    out=w_raw[parity, degree][:],
-                    in_=weights[parity][degree].rearrange("(p h) k -> p (h k)", h=2),
+                    out=raw[piece][:],
+                    in_=weights[s][i].rearrange("(p h) k -> p (h k)", h=2),
                 )
 
         ident = keep.tile([P, P], F32, name="ident")
         make_identity(nc, ident[:])
 
-        g_grouped = keep.tile([P, 4 * ROWS], BF16, name="g_grouped", align_bytes=64)
-        g_codes = keep.tile([P, ROWS], U32, name="g_codes", align_bytes=64)
-        g_scales = keep.tile([P, ROWS], U8, name="g_scales", align_bytes=64)
-        g_words = g_grouped[:].bitcast(F32).rearrange("q (g r u) -> q g r u", r=P, u=2)
-        items = ITEMS // 2
-        for half in range(2):
-            g_flip = flipped.tile([P, 2, 2 * P], F32, name="g_flip", tag="flip")
-            for t in range(2):
-                for u in range(2):
-                    nc.tensor.transpose(
-                        g_flip[:, u, P * t : P * t + P],
-                        g_raw[:, 2 * half + t, :].bitcast(F32)[:, P * u : P * u + P],
-                        ident[:],
-                    )
-            by_row = g_flip[:].rearrange("q u (n s c) -> q u n s c", s=PARITIES, c=COMPONENTS)
-            for group, (parity, pair) in enumerate(GROUPS):
-                for side, c0, w, r0 in group_layout(pair):
-                    src = by_row[:, :, :, parity, c0 : c0 + w].rearrange("q u n w -> q n w u")
-                    r1 = r0 + half * items * w
-                    dst = g_words[:, group, r1 : r1 + items * w, :].rearrange("q (n w) u -> q n w u", w=w)
-                    if half == 0:
-                        nc.vector.tensor_copy(out=dst, in_=src)
-                    else:
-                        nc.scalar.copy(out=dst, in_=src)
-        nc.vector.quantize_mx(out=g_codes[:].bitcast(E5M2X4), scales=g_scales[:], in_=g_grouped[:])
+        by_component = ident[:].rearrange("p (n j) -> p n j", j=HALF)
+        chooser = {}
+        for h, cut in ((HIGH, 1), (LOW, 4)):
+            first = keep.tile([P, 1], F32, name="first_%d" % h)
+            second = keep.tile([P, 1], F32, name="second_%d" % h)
+            nc.vector.tensor_reduce(out=first[:], in_=by_component[:, :, :cut], axis=AXES, op=ADD)
+            nc.vector.tensor_reduce(out=second[:], in_=by_component[:, :, cut:], axis=AXES, op=ADD)
+            chooser[h] = (first, second)
 
-        w_codes = {}
-        w_scales = {}
+        g_codes = {}
+        g_scales = {}
+        zero_codes = {}
+        w_codes = []
+        w_scales = []
+        for s in range(PARITIES):
+            zero_codes[s] = keep.tile([P, P], U32, name="zero_codes_%d" % s, align_bytes=64)
+            nc.gpsimd.memset(zero_codes[s][:], 0)
+            w_codes.append(keep.tile([P, DEGREES * FI], U32, name="w_codes_%d" % s, align_bytes=64))
+            w_scales.append(keep.tile([P, DEGREES * FI], U8, name="w_scales_%d" % s, align_bytes=64))
 
-        def quantise_weights(group):
-            parity, pair = GROUPS[group]
-            w_grouped = keep.tile([P, 2, 4 * FI], BF16, name="w_grouped_%d" % group, align_bytes=64)
-            w_codes[group] = keep.tile([P, 2, FI], U32, name="w_codes_%d" % group, align_bytes=64)
-            w_scales[group] = keep.tile([P, 2, FI], U8, name="w_scales_%d" % group, align_bytes=64)
-            for side, degree in enumerate(pair):
-                w_flip = flipped.tile([P, 4, P], F32, name="w_flip", tag="flip")
-                for a in range(4):
-                    nc.tensor.transpose(
-                        w_flip[:, a, :],
-                        w_raw[parity, degree][:].bitcast(F32)[:, P * a : P * a + P],
-                        ident[:],
-                    )
-                nc.scalar.copy(
-                    out=w_grouped[:, side, :].bitcast(F32).rearrange("q (p a) -> q p a", a=4),
-                    in_=w_flip[:].rearrange("q a p -> q p a"),
-                )
+        grouped = {}
+
+        def turn(piece):
+            kind, s, i = piece
+            words = raw[piece][:].bitcast(F32)
+            parts = 2 if kind == "g" else 4
+            flip = flipped.tile([P, parts, P], F32, name="flip_%s_%d_%d" % piece, tag="flip")
+            for a in range(parts):
+                nc.tensor.transpose(flip[:, a, :], words[:, P * a : P * a + P], ident[:])
+            grouped[piece] = keep.tile([P, 2 * parts * P], BF16, name="grouped_%s_%d_%d" % piece, align_bytes=64)
+            dst = grouped[piece][:].bitcast(F32).rearrange("q (p a) -> q p a", a=parts)
+            src = flip[:].rearrange("q a p -> q p a")
+            if kind == "g":
+                nc.vector.tensor_copy(out=dst, in_=src)
+            else:
+                nc.scalar.copy(out=dst, in_=src)
+
+        def quantise(piece):
+            kind, s, i = piece
+            if kind == "g":
+                codes = keep.tile([P, P], U32, name="g_codes_%d_%d" % (s, i), align_bytes=64)
+                scales = keep.tile([P, P], U8, name="g_scales_%d_%d" % (s, i), align_bytes=64)
+                nc.vector.quantize_mx(out=codes[:].bitcast(E5M2X4), scales=scales[:], in_=grouped[piece][:])
+                g_codes[s, i] = codes
+                g_scales[s, i] = scales
+                if i == LOW:
+                    here = codes[:].rearrange("q (n j) -> q n j", j=HALF)[:, :, 0]
+                    there = zero_codes[s][:].rearrange("q (n j) -> q n j", j=HALF)[:, :, 0]
+                    nc.gpsimd.tensor_copy(out=there, in_=here)
+                    nc.gpsimd.memset(here, 0)
+            else:
+                cols = slice(FI * i, FI * i + FI)
                 nc.vector.quantize_mx(
-                    out=w_codes[group][:, side, :].bitcast(E4M3X4),
-                    scales=w_scales[group][:, side, :],
-                    in_=w_grouped[:, side, :],
+                    out=w_codes[s][:, cols].bitcast(E4M3X4), scales=w_scales[s][:, cols], in_=grouped[piece][:]
                 )
 
-        def multiply(group):
-            parity, pair = GROUPS[group]
-            acc = sums.tile([P, 2, FI], F32, name="acc")
-            nc.tensor.matmul_mx(
-                out=acc[:].rearrange("r s f -> r (s f)"),
-                lhsT=g_codes[:, P * group : P * group + P].bitcast(E5M2X4),
-                lhsT_scale=g_scales[:, P * group : P * group + P],
-                rhs=w_codes[group][:].rearrange("q s f -> q (s f)").bitcast(E4M3X4),
-                rhs_scale=w_scales[group][:].rearrange("q s f -> q (s f)"),
-                start=True,
-                stop=True,
-            )
-            result = keep.tile([P, 2, FI], F32, name="result_%d" % group)
-            for side in range(2):
-                if group % 2 == 0:
-                    nc.vector.tensor_copy(out=result[:, side, :], in_=acc[:, side, :])
-                else:
-                    nc.scalar.copy(out=result[:, side, :], in_=acc[:, side, :])
-                for block_side, c0, w, r0 in group_layout(pair):
-                    if block_side == side:
-                        nc.sync.dma_start(
-                            out=out[:, parity, c0 : c0 + w, :],
-                            in_=result[r0 : r0 + ITEMS * w, side, :],
-                        )
+        acc = {}
 
-        for group in range(LOOKAHEAD):
-            quantise_weights(group)
-        for group in range(len(GROUPS)):
-            if group + LOOKAHEAD < len(GROUPS):
-                quantise_weights(group + LOOKAHEAD)
-            multiply(group)
+        def one_pass(s, h, codes, degree, start, stop):
+            cols = slice(FI * degree, FI * degree + 2 * FI)
+            nc.tensor.matmul_mx(
+                out=acc[s, h][:],
+                lhsT=codes[:].bitcast(E5M2X4),
+                lhsT_scale=g_scales[s, h][:],
+                rhs=w_codes[s][:, cols].bitcast(E4M3X4),
+                rhs_scale=w_scales[s][:, cols],
+                start=start,
+                stop=stop,
+            )
+
+        def multiply(s, h):
+            acc[s, h] = sums.tile([P, 2 * FI], F32, name="acc_%d_%d" % (s, h), tag="acc")
+            if h == HIGH:
+                one_pass(s, h, g_codes[s, h], 2, True, True)
+            else:
+                one_pass(s, h, g_codes[s, h], 1, True, False)
+                one_pass(s, h, zero_codes[s], 0, False, True)
+
+        part = {}
+
+        def choose_first(s, h):
+            part[s, h] = keep.tile([P, FI], F32, name="part_%d_%d" % (s, h))
+            nc.scalar.activation(out=part[s, h][:], in_=acc[s, h][:, :FI], func=COPY, scale=chooser[h][0][:])
+
+        def choose_second(s, h):
+            result = keep.tile([P, FI], F32, name="result_%d_%d" % (s, h))
+            nc.vector.scalar_tensor_tensor(
+                out=result[:], in0=acc[s, h][:, FI:], scalar=chooser[h][1][:], in1=part[s, h][:], op0=MULT, op1=ADD
+            )
+            nc.sync.dma_start(out=out[:, s, HALF * h : HALF * h + HALF, :], in_=result[:])
+
+        PASS_LAG = 4
+        CHOOSE_LAG = 5
+
+        complete = {}
+        for step, (kind, s, i) in enumerate(pieces):
+            if kind == "w" and i in (2, 0):
+                complete[step] = (s, HIGH if i == 2 else LOW)
+        n = len(pieces)
+        for step in range(n + CHOOSE_LAG):
+            if step < n:
+                turn(pieces[step])
+            if 1 <= step < n + 1:
+                quantise(pieces[step - 1])
+            if step - PASS_LAG in complete:
+                multiply(*complete[step - PASS_LAG])
+                choose_first(*complete[step - PASS_LAG])
+            if step - CHOOSE_LAG in complete:
+                choose_second(*complete[step - CHOOSE_LAG])

@@ -12,7 +12,8 @@ E5M2X4 = mybir.dt.float8_e5m2_x4
 COPY = mybir.ActivationFunctionType.Copy
 ADD = mybir.AluOpType.add
 MULT = mybir.AluOpType.mult
-AXES = mybir.AxisListType.XY
+AXIS_X = mybir.AxisListType.X
+AXES_XY = mybir.AxisListType.XY
 
 P = 128
 ITEMS = 16
@@ -22,9 +23,16 @@ DEGREES = 4
 FI = 256
 FO = 512
 ROWS = ITEMS * PARITIES * COMPONENTS
+RUN = 8
 
-HALF = COMPONENTS // 2
-LOW, HIGH = 0, 1
+EVEN, ODD = 0, 1
+
+GROUPS = (
+    (((EVEN, 1), (EVEN, 2)), ((1, 8),)),
+    (((EVEN, 3), (ODD, 0)), ((9, 8),)),
+    (((ODD, 3), (EVEN, 0)), ((25, 4), (29, 2), (31, 1), (0, 1))),
+    (((ODD, 1), (ODD, 2)), ((17, 8),)),
+)
 
 FLOPS = 2 * ROWS * FO * FI
 BYTES = 2 * (2 * DEGREES * FI * FO) + 2 * ROWS * FO + 4 * ROWS * FI
@@ -36,135 +44,143 @@ def tile_dense_pa_s_kernel(tc, x, W_e, W_o, b, grad_out, out):
     with ExitStack() as ctx:
         ctx.enter_context(tc.manual_schedule())
         keep = ctx.enter_context(tc.tile_pool(name="keep", bufs=1))
-        flipped = ctx.enter_context(tc.psum_pool(name="flipped", bufs=5))
-        sums = ctx.enter_context(tc.psum_pool(name="sums", bufs=3))
+        flipped = ctx.enter_context(tc.psum_pool(name="flipped", bufs=6))
+        sums = ctx.enter_context(tc.psum_pool(name="sums", bufs=2))
+
+        g_rows = grad_out.rearrange("n s c k -> n (s c) k")
+        out_rows = out.rearrange("n s c f -> n (s c) f")
 
         pieces = []
-        for s in range(PARITIES):
-            pieces += [("g", s, HIGH), ("w", s, 3), ("w", s, 2), ("g", s, LOW), ("w", s, 1), ("w", s, 0)]
+        for group in range(len(GROUPS)):
+            pieces += [(group, None), (group, 0), (group, 1)]
 
         raw = {}
-        for piece in pieces:
-            kind, s, i = piece
-            if kind == "g":
-                raw[piece] = keep.tile([P, FO], BF16, name="g_raw_%d_%d" % (s, i))
-                nc.sync.dma_start(out=raw[piece][:], in_=grad_out[:, s, HALF * i : HALF * i + HALF, :])
+        for group, side in pieces:
+            if side is None:
+                raw[group, side] = keep.tile([P, FO], BF16, name="g_raw_%d" % group)
+                r0 = 0
+                for first, w in GROUPS[group][1]:
+                    nc.sync.dma_start(
+                        out=raw[group, side][r0 : r0 + ITEMS * w, :],
+                        in_=g_rows[:, first : first + w, :],
+                    )
+                    r0 += ITEMS * w
             else:
-                raw[piece] = keep.tile([P, 2 * FO], BF16, name="w_raw_%d_%d" % (s, i))
+                parity, degree = GROUPS[group][0][side]
+                raw[group, side] = keep.tile([P, 2 * FO], BF16, name="w_raw_%d_%d" % (group, side))
                 nc.sync.dma_start(
-                    out=raw[piece][:],
-                    in_=weights[s][i].rearrange("(p h) k -> p (h k)", h=2),
+                    out=raw[group, side][:],
+                    in_=weights[parity][degree].rearrange("(p h) k -> p (h k)", h=2),
                 )
 
         ident = keep.tile([P, P], F32, name="ident")
         make_identity(nc, ident[:])
 
-        by_component = ident[:].rearrange("p (n j) -> p n j", j=HALF)
-        chooser = {}
-        for h, cut in ((HIGH, 1), (LOW, 4)):
-            first = keep.tile([P, 1], F32, name="first_%d" % h)
-            second = keep.tile([P, 1], F32, name="second_%d" % h)
-            nc.vector.tensor_reduce(out=first[:], in_=by_component[:, :, :cut], axis=AXES, op=ADD)
-            nc.vector.tensor_reduce(out=second[:], in_=by_component[:, :, cut:], axis=AXES, op=ADD)
-            chooser[h] = (first, second)
-
-        g_codes = {}
-        g_scales = {}
-        zero_codes = {}
-        w_codes = []
-        w_scales = []
-        for s in range(PARITIES):
-            zero_codes[s] = keep.tile([P, P], U32, name="zero_codes_%d" % s, align_bytes=64)
-            nc.gpsimd.memset(zero_codes[s][:], 0)
-            w_codes.append(keep.tile([P, DEGREES * FI], U32, name="w_codes_%d" % s, align_bytes=64))
-            w_scales.append(keep.tile([P, DEGREES * FI], U8, name="w_scales_%d" % s, align_bytes=64))
+        by_run = ident[:].rearrange("p (n j) -> p n j", j=RUN)
+        chooser = []
+        for group, (sides, runs) in enumerate(GROUPS):
+            mine = 2 * sides[0][1] + 1
+            first = keep.tile([P, 1], F32, name="first_%d" % group)
+            second = keep.tile([P, 1], F32, name="second_%d" % group)
+            if len(runs) == 1:
+                nc.vector.tensor_reduce(out=first[:], in_=by_run[:, :, :mine], axis=AXES_XY, op=ADD)
+                nc.vector.tensor_reduce(out=second[:], in_=by_run[:, :, mine:], axis=AXES_XY, op=ADD)
+            else:
+                nc.vector.tensor_reduce(out=first[:], in_=ident[:, : ITEMS * mine], axis=AXIS_X, op=ADD)
+                nc.vector.tensor_reduce(out=second[:], in_=ident[:, ITEMS * mine :], axis=AXIS_X, op=ADD)
+            chooser.append((first, second))
 
         grouped = {}
+        codes = {}
+        scales = {}
+        for group in range(len(GROUPS)):
+            codes[group, None] = keep.tile([P, P], U32, name="g_codes_%d" % group, align_bytes=64)
+            scales[group, None] = keep.tile([P, P], U8, name="g_scales_%d" % group, align_bytes=64)
+            pair_codes = keep.tile([P, 2, FI], U32, name="w_codes_%d" % group, align_bytes=64)
+            pair_scales = keep.tile([P, 2, FI], U8, name="w_scales_%d" % group, align_bytes=64)
+            codes[group, "pair"] = pair_codes
+            scales[group, "pair"] = pair_scales
 
-        def turn(piece):
-            kind, s, i = piece
-            words = raw[piece][:].bitcast(F32)
-            parts = 2 if kind == "g" else 4
-            flip = flipped.tile([P, parts, P], F32, name="flip_%s_%d_%d" % piece, tag="flip")
+        def turn(group, side):
+            words = raw[group, side][:].bitcast(F32)
+            parts = 2 if side is None else 4
+            flip = flipped.tile([P, parts, P], F32, name="flip", tag="flip")
             for a in range(parts):
                 nc.tensor.transpose(flip[:, a, :], words[:, P * a : P * a + P], ident[:])
-            grouped[piece] = keep.tile([P, 2 * parts * P], BF16, name="grouped_%s_%d_%d" % piece, align_bytes=64)
-            dst = grouped[piece][:].bitcast(F32).rearrange("q (p a) -> q p a", a=parts)
+            label = "g_grouped_%d" % group if side is None else "w_grouped_%d_%d" % (group, side)
+            grouped[group, side] = keep.tile([P, 2 * parts * P], BF16, name=label, align_bytes=64)
+            dst = grouped[group, side][:].bitcast(F32).rearrange("q (p a) -> q p a", a=parts)
             src = flip[:].rearrange("q a p -> q p a")
-            if kind == "g":
+            if side is None:
                 nc.vector.tensor_copy(out=dst, in_=src)
             else:
                 nc.scalar.copy(out=dst, in_=src)
 
-        def quantise(piece):
-            kind, s, i = piece
-            if kind == "g":
-                codes = keep.tile([P, P], U32, name="g_codes_%d_%d" % (s, i), align_bytes=64)
-                scales = keep.tile([P, P], U8, name="g_scales_%d_%d" % (s, i), align_bytes=64)
-                nc.vector.quantize_mx(out=codes[:].bitcast(E5M2X4), scales=scales[:], in_=grouped[piece][:])
-                g_codes[s, i] = codes
-                g_scales[s, i] = scales
-                if i == LOW:
-                    here = codes[:].rearrange("q (n j) -> q n j", j=HALF)[:, :, 0]
-                    there = zero_codes[s][:].rearrange("q (n j) -> q n j", j=HALF)[:, :, 0]
-                    nc.gpsimd.tensor_copy(out=there, in_=here)
-                    nc.gpsimd.memset(here, 0)
-            else:
-                cols = slice(FI * i, FI * i + FI)
+        def quantise(group, side):
+            if side is None:
                 nc.vector.quantize_mx(
-                    out=w_codes[s][:, cols].bitcast(E4M3X4), scales=w_scales[s][:, cols], in_=grouped[piece][:]
+                    out=codes[group, None][:].bitcast(E5M2X4),
+                    scales=scales[group, None][:],
+                    in_=grouped[group, side][:],
+                )
+            else:
+                nc.vector.quantize_mx(
+                    out=codes[group, "pair"][:, side, :].bitcast(E4M3X4),
+                    scales=scales[group, "pair"][:, side, :],
+                    in_=grouped[group, side][:],
                 )
 
         acc = {}
-
-        def one_pass(s, h, codes, degree, start, stop):
-            cols = slice(FI * degree, FI * degree + 2 * FI)
-            nc.tensor.matmul_mx(
-                out=acc[s, h][:],
-                lhsT=codes[:].bitcast(E5M2X4),
-                lhsT_scale=g_scales[s, h][:],
-                rhs=w_codes[s][:, cols].bitcast(E4M3X4),
-                rhs_scale=w_scales[s][:, cols],
-                start=start,
-                stop=stop,
-            )
-
-        def multiply(s, h):
-            acc[s, h] = sums.tile([P, 2 * FI], F32, name="acc_%d_%d" % (s, h), tag="acc")
-            if h == HIGH:
-                one_pass(s, h, g_codes[s, h], 2, True, True)
-            else:
-                one_pass(s, h, g_codes[s, h], 1, True, False)
-                one_pass(s, h, zero_codes[s], 0, False, True)
-
         part = {}
 
-        def choose_first(s, h):
-            part[s, h] = keep.tile([P, FI], F32, name="part_%d_%d" % (s, h))
-            nc.scalar.activation(out=part[s, h][:], in_=acc[s, h][:, :FI], func=COPY, scale=chooser[h][0][:])
-
-        def choose_second(s, h):
-            result = keep.tile([P, FI], F32, name="result_%d_%d" % (s, h))
-            nc.vector.scalar_tensor_tensor(
-                out=result[:], in0=acc[s, h][:, FI:], scalar=chooser[h][1][:], in1=part[s, h][:], op0=MULT, op1=ADD
+        def multiply(group):
+            acc[group] = sums.tile([P, 2, FI], F32, name="acc", tag="acc")
+            nc.tensor.matmul_mx(
+                out=acc[group][:].rearrange("r s f -> r (s f)"),
+                lhsT=codes[group, None][:].bitcast(E5M2X4),
+                lhsT_scale=scales[group, None][:],
+                rhs=codes[group, "pair"][:].rearrange("q s f -> q (s f)").bitcast(E4M3X4),
+                rhs_scale=scales[group, "pair"][:].rearrange("q s f -> q (s f)"),
+                start=True,
+                stop=True,
             )
-            nc.sync.dma_start(out=out[:, s, HALF * h : HALF * h + HALF, :], in_=result[:])
+
+        def choose_first(group):
+            part[group] = keep.tile([P, FI], F32, name="part_%d" % group)
+            nc.scalar.activation(
+                out=part[group][:], in_=acc[group][:, 0, :], func=COPY, scale=chooser[group][0][:]
+            )
+
+        def choose_second(group):
+            result = keep.tile([P, FI], F32, name="result_%d" % group)
+            nc.vector.scalar_tensor_tensor(
+                out=result[:],
+                in0=acc[group][:, 1, :],
+                scalar=chooser[group][1][:],
+                in1=part[group][:],
+                op0=MULT,
+                op1=ADD,
+            )
+            r0 = 0
+            for first, w in GROUPS[group][1]:
+                nc.sync.dma_start(out=out_rows[:, first : first + w, :], in_=result[r0 : r0 + ITEMS * w, :])
+                r0 += ITEMS * w
 
         PASS_LAG = 4
         CHOOSE_LAG = 5
-
         complete = {}
-        for step, (kind, s, i) in enumerate(pieces):
-            if kind == "w" and i in (2, 0):
-                complete[step] = (s, HIGH if i == 2 else LOW)
+        for step, (group, side) in enumerate(pieces):
+            complete[group] = step
         n = len(pieces)
         for step in range(n + CHOOSE_LAG):
             if step < n:
-                turn(pieces[step])
+                turn(*pieces[step])
             if 1 <= step < n + 1:
-                quantise(pieces[step - 1])
-            if step - PASS_LAG in complete:
-                multiply(*complete[step - PASS_LAG])
-                choose_first(*complete[step - PASS_LAG])
-            if step - CHOOSE_LAG in complete:
-                choose_second(*complete[step - CHOOSE_LAG])
+                quantise(*pieces[step - 1])
+            for group in range(len(GROUPS)):
+                if step == complete[group] + PASS_LAG:
+                    multiply(group)
+                    choose_first(group)
+            for group in range(len(GROUPS)):
+                if step == complete[group] + CHOOSE_LAG:
+                    choose_second(group)

@@ -12,7 +12,6 @@ E5M2X4 = mybir.dt.float8_e5m2_x4
 COPY = mybir.ActivationFunctionType.Copy
 ADD = mybir.AluOpType.add
 MULT = mybir.AluOpType.mult
-AXIS_X = mybir.AxisListType.X
 AXES_XY = mybir.AxisListType.XY
 
 P = 128
@@ -30,9 +29,10 @@ EVEN, ODD = 0, 1
 GROUPS = (
     (((EVEN, 1), (EVEN, 2)), ((1, 8),)),
     (((EVEN, 3), (ODD, 0)), ((9, 8),)),
-    (((ODD, 3), (EVEN, 0)), ((25, 4), (29, 2), (31, 1), (0, 1))),
     (((ODD, 1), (ODD, 2)), ((17, 8),)),
+    (((ODD, 3), (EVEN, 0)), ((25, 4), (29, 2), (31, 1), (0, 1))),
 )
+LAST = len(GROUPS) - 1
 
 FLOPS = 2 * ROWS * FO * FI
 BYTES = 2 * (2 * DEGREES * FI * FO) + 2 * ROWS * FO + 4 * ROWS * FI
@@ -44,8 +44,8 @@ def tile_dense_pa_s_kernel(tc, x, W_e, W_o, b, grad_out, out):
     with ExitStack() as ctx:
         ctx.enter_context(tc.manual_schedule())
         keep = ctx.enter_context(tc.tile_pool(name="keep", bufs=1))
-        flipped = ctx.enter_context(tc.psum_pool(name="flipped", bufs=6))
-        sums = ctx.enter_context(tc.psum_pool(name="sums", bufs=2))
+        flipped = ctx.enter_context(tc.psum_pool(name="flipped", bufs=5))
+        sums = ctx.enter_context(tc.psum_pool(name="sums", bufs=3))
 
         g_rows = grad_out.rearrange("n s c k -> n (s c) k")
         out_rows = out.rearrange("n s c f -> n (s c) f")
@@ -73,33 +73,33 @@ def tile_dense_pa_s_kernel(tc, x, W_e, W_o, b, grad_out, out):
                     in_=weights[parity][degree].rearrange("(p h) k -> p (h k)", h=2),
                 )
 
+        zeros = keep.tile([P, P], F32, name="zeros")
+        nc.vector.memset(zeros[:], 0.0)
+        idle = sums.tile([P, 3, P], F32, name="idle", tag="acc")
+        for i in range(3):
+            nc.tensor.matmul(idle[:, i, :], lhsT=zeros[:], rhs=zeros[:], start=True, stop=True)
+
         ident = keep.tile([P, P], F32, name="ident")
         make_identity(nc, ident[:])
 
         by_run = ident[:].rearrange("p (n j) -> p n j", j=RUN)
         chooser = []
-        for group, (sides, runs) in enumerate(GROUPS):
-            mine = 2 * sides[0][1] + 1
+        for group in range(LAST):
+            mine = 2 * GROUPS[group][0][0][1] + 1
             first = keep.tile([P, 1], F32, name="first_%d" % group)
             second = keep.tile([P, 1], F32, name="second_%d" % group)
-            if len(runs) == 1:
-                nc.vector.tensor_reduce(out=first[:], in_=by_run[:, :, :mine], axis=AXES_XY, op=ADD)
-                nc.vector.tensor_reduce(out=second[:], in_=by_run[:, :, mine:], axis=AXES_XY, op=ADD)
-            else:
-                nc.vector.tensor_reduce(out=first[:], in_=ident[:, : ITEMS * mine], axis=AXIS_X, op=ADD)
-                nc.vector.tensor_reduce(out=second[:], in_=ident[:, ITEMS * mine :], axis=AXIS_X, op=ADD)
+            nc.vector.tensor_reduce(out=first[:], in_=by_run[:, :, :mine], axis=AXES_XY, op=ADD)
+            nc.vector.tensor_reduce(out=second[:], in_=by_run[:, :, mine:], axis=AXES_XY, op=ADD)
             chooser.append((first, second))
 
         grouped = {}
-        codes = {}
-        scales = {}
+        g_codes = {}
+        g_scales = {}
         for group in range(len(GROUPS)):
-            codes[group, None] = keep.tile([P, P], U32, name="g_codes_%d" % group, align_bytes=64)
-            scales[group, None] = keep.tile([P, P], U8, name="g_scales_%d" % group, align_bytes=64)
-            pair_codes = keep.tile([P, 2, FI], U32, name="w_codes_%d" % group, align_bytes=64)
-            pair_scales = keep.tile([P, 2, FI], U8, name="w_scales_%d" % group, align_bytes=64)
-            codes[group, "pair"] = pair_codes
-            scales[group, "pair"] = pair_scales
+            g_codes[group] = keep.tile([P, P], U32, name="g_codes_%d" % group, align_bytes=64)
+            g_scales[group] = keep.tile([P, P], U8, name="g_scales_%d" % group, align_bytes=64)
+        w_codes = keep.tile([P, 2 * len(GROUPS) * FI], U32, name="w_codes", align_bytes=64)
+        w_scales = keep.tile([P, 2 * len(GROUPS) * FI], U8, name="w_scales", align_bytes=64)
 
         def turn(group, side):
             words = raw[group, side][:].bitcast(F32)
@@ -111,7 +111,7 @@ def tile_dense_pa_s_kernel(tc, x, W_e, W_o, b, grad_out, out):
             grouped[group, side] = keep.tile([P, 2 * parts * P], BF16, name=label, align_bytes=64)
             dst = grouped[group, side][:].bitcast(F32).rearrange("q (p a) -> q p a", a=parts)
             src = flip[:].rearrange("q a p -> q p a")
-            if side is None:
+            if side is None or (group, side) == (1, 1):
                 nc.vector.tensor_copy(out=dst, in_=src)
             else:
                 nc.scalar.copy(out=dst, in_=src)
@@ -119,31 +119,33 @@ def tile_dense_pa_s_kernel(tc, x, W_e, W_o, b, grad_out, out):
         def quantise(group, side):
             if side is None:
                 nc.vector.quantize_mx(
-                    out=codes[group, None][:].bitcast(E5M2X4),
-                    scales=scales[group, None][:],
-                    in_=grouped[group, side][:],
+                    out=g_codes[group][:].bitcast(E5M2X4), scales=g_scales[group][:], in_=grouped[group, side][:]
                 )
             else:
+                cols = slice(FI * (2 * group + side), FI * (2 * group + side) + FI)
                 nc.vector.quantize_mx(
-                    out=codes[group, "pair"][:, side, :].bitcast(E4M3X4),
-                    scales=scales[group, "pair"][:, side, :],
-                    in_=grouped[group, side][:],
+                    out=w_codes[:, cols].bitcast(E4M3X4), scales=w_scales[:, cols], in_=grouped[group, side][:]
                 )
+
+        def one_pass(group, first_weight):
+            acc = sums.tile([P, 2, FI], F32, name="acc", tag="acc")
+            cols = slice(FI * first_weight, FI * first_weight + 2 * FI)
+            nc.tensor.matmul_mx(
+                out=acc[:].rearrange("r s f -> r (s f)"),
+                lhsT=g_codes[group][:].bitcast(E5M2X4),
+                lhsT_scale=g_scales[group][:],
+                rhs=w_codes[:, cols].bitcast(E4M3X4),
+                rhs_scale=w_scales[:, cols],
+                start=True,
+                stop=True,
+            )
+            return acc
 
         acc = {}
         part = {}
 
         def multiply(group):
-            acc[group] = sums.tile([P, 2, FI], F32, name="acc", tag="acc")
-            nc.tensor.matmul_mx(
-                out=acc[group][:].rearrange("r s f -> r (s f)"),
-                lhsT=codes[group, None][:].bitcast(E5M2X4),
-                lhsT_scale=scales[group, None][:],
-                rhs=codes[group, "pair"][:].rearrange("q s f -> q (s f)").bitcast(E4M3X4),
-                rhs_scale=scales[group, "pair"][:].rearrange("q s f -> q (s f)"),
-                start=True,
-                stop=True,
-            )
+            acc[group] = one_pass(group, 2 * group)
 
         def choose_first(group):
             part[group] = keep.tile([P, FI], F32, name="part_%d" % group)
@@ -161,26 +163,39 @@ def tile_dense_pa_s_kernel(tc, x, W_e, W_o, b, grad_out, out):
                 op0=MULT,
                 op1=ADD,
             )
-            r0 = 0
-            for first, w in GROUPS[group][1]:
-                nc.sync.dma_start(out=out_rows[:, first : first + w, :], in_=result[r0 : r0 + ITEMS * w, :])
-                r0 += ITEMS * w
+            first, w = GROUPS[group][1][0]
+            nc.sync.dma_start(out=out_rows[:, first : first + w, :], in_=result[:])
 
-        PASS_LAG = 4
-        CHOOSE_LAG = 5
+        PASS_LAG = 5
+        FIRST_LAG = 5
+        SECOND_LAG = 6
         complete = {}
         for step, (group, side) in enumerate(pieces):
             complete[group] = step
         n = len(pieces)
-        for step in range(n + CHOOSE_LAG):
+        for step in range(n + 3):
             if step < n:
                 turn(*pieces[step])
             if 1 <= step < n + 1:
                 quantise(*pieces[step - 1])
-            for group in range(len(GROUPS)):
+            for group in range(LAST):
                 if step == complete[group] + PASS_LAG:
                     multiply(group)
+                if step == complete[group] + FIRST_LAG:
                     choose_first(group)
-            for group in range(len(GROUPS)):
-                if step == complete[group] + CHOOSE_LAG:
+                if step == complete[group] + SECOND_LAG:
                     choose_second(group)
+
+        r0 = 0
+        for side in range(2):
+            last_acc = one_pass(LAST, 2 * LAST + side - 1)
+            last_result = keep.tile([P, FI], F32, name="last_result_%d" % side)
+            if side == 0:
+                nc.scalar.copy(out=last_result[:], in_=last_acc[:, 1, :])
+                runs = GROUPS[LAST][1][:3]
+            else:
+                nc.vector.tensor_copy(out=last_result[:], in_=last_acc[:, 1, :])
+                runs = GROUPS[LAST][1][3:]
+            for first, w in runs:
+                nc.sync.dma_start(out=out_rows[:, first : first + w, :], in_=last_result[r0 : r0 + ITEMS * w, :])
+                r0 += ITEMS * w

@@ -73,11 +73,11 @@ def tile_dense_pa_s_kernel(tc, x, W_e, W_o, b, grad_out, out):
                     in_=weights[parity][degree].rearrange("(p h) k -> p (h k)", h=2),
                 )
 
-        zeros = keep.tile([P, P], F32, name="zeros")
-        nc.vector.memset(zeros[:], 0.0)
+        ones = keep.tile([P, P], F32, name="ones")
+        nc.vector.memset(ones[:], 1.0)
         idle = sums.tile([P, 3, P], F32, name="idle", tag="acc")
         for i in range(3):
-            nc.tensor.matmul(idle[:, i, :], lhsT=zeros[:], rhs=zeros[:], start=True, stop=True)
+            nc.tensor.matmul(idle[:, i, :], lhsT=ones[:], rhs=ones[:], start=True, stop=True)
 
         ident = keep.tile([P, P], F32, name="ident")
         make_identity(nc, ident[:])

@@ -27,10 +27,10 @@ RUN = 8
 EVEN, ODD = 0, 1
 
 GROUPS = (
-    (((EVEN, 1), (EVEN, 2)), ((1, 8),)),
-    (((EVEN, 3), (ODD, 0)), ((9, 8),)),
-    (((ODD, 1), (ODD, 2)), ((17, 8),)),
-    (((ODD, 3), (EVEN, 0)), ((25, 4), (29, 2), (31, 1), (0, 1))),
+    (((EVEN, 1), (EVEN, 2)), ((1, 8, 0),)),
+    (((EVEN, 3), (ODD, 0)), ((9, 8, 0),)),
+    (((ODD, 1), (ODD, 2)), ((17, 8, 0),)),
+    (((ODD, 3), (EVEN, 0)), ((25, 4, 0), (29, 2, 1), (31, 1, 3), (0, 1, 7))),
 )
 LAST = len(GROUPS) - 1
 
@@ -58,13 +58,11 @@ def tile_dense_pa_s_kernel(tc, x, W_e, W_o, b, grad_out, out):
         for group, side in pieces:
             if side is None:
                 raw[group, side] = keep.tile([P, FO], BF16, name="g_raw_%d" % group)
-                r0 = 0
-                for first, w in GROUPS[group][1]:
+                for first, w, start in GROUPS[group][1]:
                     nc.sync.dma_start(
-                        out=raw[group, side][r0 : r0 + ITEMS * w, :],
+                        out=raw[group, side][start : P : RUN // w, :],
                         in_=g_rows[:, first : first + w, :],
                     )
-                    r0 += ITEMS * w
             else:
                 parity, degree = GROUPS[group][0][side]
                 raw[group, side] = keep.tile([P, 2 * FO], BF16, name="w_raw_%d_%d" % (group, side))
@@ -163,7 +161,7 @@ def tile_dense_pa_s_kernel(tc, x, W_e, W_o, b, grad_out, out):
                 op0=MULT,
                 op1=ADD,
             )
-            first, w = GROUPS[group][1][0]
+            first, w, start = GROUPS[group][1][0]
             nc.sync.dma_start(out=out_rows[:, first : first + w, :], in_=result[:])
 
         PASS_LAG = 5
@@ -186,7 +184,6 @@ def tile_dense_pa_s_kernel(tc, x, W_e, W_o, b, grad_out, out):
                 if step == complete[group] + SECOND_LAG:
                     choose_second(group)
 
-        r0 = 0
         for side in range(2):
             last_acc = one_pass(LAST, 2 * LAST + side - 1)
             last_result = keep.tile([P, FI], F32, name="last_result_%d" % side)
@@ -196,6 +193,5 @@ def tile_dense_pa_s_kernel(tc, x, W_e, W_o, b, grad_out, out):
             else:
                 nc.vector.tensor_copy(out=last_result[:], in_=last_acc[:, 1, :])
                 runs = GROUPS[LAST][1][3:]
-            for first, w in runs:
-                nc.sync.dma_start(out=out_rows[:, first : first + w, :], in_=last_result[r0 : r0 + ITEMS * w, :])
-                r0 += ITEMS * w
+            for first, w, start in runs:
+                nc.sync.dma_start(out=out_rows[:, first : first + w, :], in_=last_result[start : P : RUN // w, :])

@@ -51,18 +51,26 @@ def tile_dense_pa_s_kernel(tc, x, W_e, W_o, b, grad_out, out):
         out_rows = out.rearrange("n s c f -> n (s c) f")
 
         pieces = []
-        for group in range(len(GROUPS)):
+        for group in range(LAST):
             pieces += [(group, None), (group, 0), (group, 1)]
+        pieces += [(LAST, 0), (LAST, None), (LAST, 1)]
 
         raw = {}
+        raw[LAST, None] = keep.tile([P, FO], BF16, name="g_raw_%d" % LAST)
+
+        def load_runs(group, runs):
+            for first, w, start in runs:
+                nc.sync.dma_start(
+                    out=raw[group, None][start : P : RUN // w, :],
+                    in_=g_rows[:, first : first + w, :],
+                )
+
         for group, side in pieces:
-            if side is None:
-                raw[group, side] = keep.tile([P, FO], BF16, name="g_raw_%d" % group)
-                for first, w, start in GROUPS[group][1]:
-                    nc.sync.dma_start(
-                        out=raw[group, side][start : P : RUN // w, :],
-                        in_=g_rows[:, first : first + w, :],
-                    )
+            if side is None and group < LAST:
+                raw[group, None] = keep.tile([P, FO], BF16, name="g_raw_%d" % group)
+                load_runs(group, GROUPS[group][1])
+            elif side is None:
+                load_runs(LAST, GROUPS[LAST][1][:1])
             else:
                 parity, degree = GROUPS[group][0][side]
                 raw[group, side] = keep.tile([P, 2 * FO], BF16, name="w_raw_%d_%d" % (group, side))
@@ -70,6 +78,8 @@ def tile_dense_pa_s_kernel(tc, x, W_e, W_o, b, grad_out, out):
                     out=raw[group, side][:],
                     in_=weights[parity][degree].rearrange("(p h) k -> p (h k)", h=2),
                 )
+                if side == 1 and group < LAST:
+                    load_runs(LAST, GROUPS[LAST][1][LAST - group : LAST - group + 1])
 
         ones = keep.tile([P, P], F32, name="ones")
         nc.vector.memset(ones[:], 1.0)
@@ -109,7 +119,7 @@ def tile_dense_pa_s_kernel(tc, x, W_e, W_o, b, grad_out, out):
             grouped[group, side] = keep.tile([P, 2 * parts * P], BF16, name=label, align_bytes=64)
             dst = grouped[group, side][:].bitcast(F32).rearrange("q (p a) -> q p a", a=parts)
             src = flip[:].rearrange("q a p -> q p a")
-            if side is None or (group, side) == (1, 1):
+            if side is None or (group, side) == (0, 1):
                 nc.vector.tensor_copy(out=dst, in_=src)
             else:
                 nc.scalar.copy(out=dst, in_=src)

from contextlib import ExitStack

import concourse.mybir as mybir
from concourse.masks import make_identity

F32 = mybir.dt.float32
BF16 = mybir.dt.bfloat16
U32 = mybir.dt.uint32
U8 = mybir.dt.uint8
E4M3X4 = mybir.dt.float8_e4m3fn_x4
E5M2X4 = mybir.dt.float8_e5m2_x4
COPY = mybir.ActivationFunctionType.Copy
ADD = mybir.AluOpType.add
MULT = mybir.AluOpType.mult
AXES_XY = mybir.AxisListType.XY

P = 128
ITEMS = 16
PARITIES = 2
COMPONENTS = 16
DEGREES = 4
FI = 256
FO = 512
ROWS = ITEMS * PARITIES * COMPONENTS
RUN = 8

EVEN, ODD = 0, 1

GROUPS = (
    (((EVEN, 1), (EVEN, 2)), ((1, 8, 0),)),
    (((EVEN, 3), (ODD, 0)), ((9, 8, 0),)),
    (((ODD, 1), (ODD, 2)), ((17, 8, 0),)),
    (((ODD, 3), (EVEN, 0)), ((25, 4, 0), (29, 2, 1), (31, 1, 3), (0, 1, 7))),
)
LAST = len(GROUPS) - 1

FLOPS = 2 * ROWS * FO * FI
BYTES = 2 * (2 * DEGREES * FI * FO) + 2 * ROWS * FO + 4 * ROWS * FI


def tile_dense_pa_s_kernel(tc, x, W_e, W_o, b, grad_out, out):
    nc = tc.nc
    weights = (W_e, W_o)
    with ExitStack() as ctx:
        ctx.enter_context(tc.manual_schedule())
        keep = ctx.enter_context(tc.tile_pool(name="keep", bufs=1))
        flipped = ctx.enter_context(tc.psum_pool(name="flipped", bufs=5))
        sums = ctx.enter_context(tc.psum_pool(name="sums", bufs=3))

        g_rows = grad_out.rearrange("n s c k -> n (s c) k")
        out_rows = out.rearrange("n s c f -> n (s c) f")

        pieces = []
        for group in range(LAST):
            pieces += [(group, None), (group, 0), (group, 1)]
        pieces += [(LAST, 0), (LAST, None), (LAST, 1)]

        raw = {}
        raw[LAST, None] = keep.tile([P, FO], BF16, name="g_raw_%d" % LAST)

        def load_runs(group, runs):
            for first, w, start in runs:
                nc.sync.dma_start(
                    out=raw[group, None][start : P : RUN // w, :],
                    in_=g_rows[:, first : first + w, :],
                )

        for group, side in pieces:
            if side is None and group < LAST:
                raw[group, None] = keep.tile([P, FO], BF16, name="g_raw_%d" % group)
                load_runs(group, GROUPS[group][1])
            elif side is None:
                load_runs(LAST, GROUPS[LAST][1][:1])
            else:
                parity, degree = GROUPS[group][0][side]
                raw[group, side] = keep.tile([P, 2 * FO], BF16, name="w_raw_%d_%d" % (group, side))
                nc.sync.dma_start(
                    out=raw[group, side][:],
                    in_=weights[parity][degree].rearrange("(p h) k -> p (h k)", h=2),
                )
                if side == 1 and group < LAST:
                    load_runs(LAST, GROUPS[LAST][1][LAST - group : LAST - group + 1])

        ones = keep.tile([P, P], F32, name="ones")
        nc.vector.memset(ones[:], 1.0)
        idle = sums.tile([P, 3, P], F32, name="idle", tag="acc")
        for i in range(3):
            nc.tensor.matmul(idle[:, i, :], lhsT=ones[:], rhs=ones[:], start=True, stop=True)

        ident = keep.tile([P, P], F32, name="ident")
        make_identity(nc, ident[:])

        by_run = ident[:].rearrange("p (n j) -> p n j", j=RUN)
        chooser = []
        for group in range(LAST):
            mine = 2 * GROUPS[group][0][0][1] + 1
            first = keep.tile([P, 1], F32, name="first_%d" % group)
            second = keep.tile([P, 1], F32, name="second_%d" % group)
            nc.vector.tensor_reduce(out=first[:], in_=by_run[:, :, :mine], axis=AXES_XY, op=ADD)
            nc.vector.tensor_reduce(out=second[:], in_=by_run[:, :, mine:], axis=AXES_XY, op=ADD)
            chooser.append((first, second))

        grouped = {}
        g_codes = {}
        g_scales = {}
        for group in range(len(GROUPS)):
            g_codes[group] = keep.tile([P, P], U32, name="g_codes_%d" % group, align_bytes=64)
            g_scales[group] = keep.tile([P, P], U8, name="g_scales_%d" % group, align_bytes=64)
        w_codes = keep.tile([P, 2 * len(GROUPS) * FI], U32, name="w_codes", align_bytes=64)
        w_scales = keep.tile([P, 2 * len(GROUPS) * FI], U8, name="w_scales", align_bytes=64)

        def turn(group, side):
            words = raw[group, side][:].bitcast(F32)
            parts = 2 if side is None else 4
            flip = flipped.tile([P, parts, P], F32, name="flip", tag="flip")
            for a in range(parts):
                nc.tensor.transpose(flip[:, a, :], words[:, P * a : P * a + P], ident[:])
            label = "g_grouped_%d" % group if side is None else "w_grouped_%d_%d" % (group, side)
            grouped[group, side] = keep.tile([P, 2 * parts * P], BF16, name=label, align_bytes=64)
            dst = grouped[group, side][:].bitcast(F32).rearrange("q (p a) -> q p a", a=parts)
            src = flip[:].rearrange("q a p -> q p a")
            if side is None or (group, side) == (0, 1):
                nc.vector.tensor_copy(out=dst, in_=src)
            else:
                nc.scalar.copy(out=dst, in_=src)

        def quantise(group, side):
            if side is None:
                nc.vector.quantize_mx(
                    out=g_codes[group][:].bitcast(E5M2X4), scales=g_scales[group][:], in_=grouped[group, side][:]
                )
            else:
                cols = slice(FI * (2 * group + side), FI * (2 * group + side) + FI)
                nc.vector.quantize_mx(
                    out=w_codes[:, cols].bitcast(E4M3X4), scales=w_scales[:, cols], in_=grouped[group, side][:]
                )

        def one_pass(group, first_weight):
            acc = sums.tile([P, 2, FI], F32, name="acc", tag="acc")
            cols = slice(FI * first_weight, FI * first_weight + 2 * FI)
            nc.tensor.matmul_mx(
                out=acc[:].rearrange("r s f -> r (s f)"),
                lhsT=g_codes[group][:].bitcast(E5M2X4),
                lhsT_scale=g_scales[group][:],
                rhs=w_codes[:, cols].bitcast(E4M3X4),
                rhs_scale=w_scales[:, cols],
                start=True,
                stop=True,
            )
            return acc

        acc = {}
        part = {}

        def multiply(group):
            acc[group] = one_pass(group, 2 * group)

        def choose_first(group):
            part[group] = keep.tile([P, FI], F32, name="part_%d" % group)
            nc.scalar.activation(
                out=part[group][:], in_=acc[group][:, 0, :], func=COPY, scale=chooser[group][0][:]
            )

        def choose_second(group):
            result = keep.tile([P, FI], F32, name="result_%d" % group)
            nc.vector.scalar_tensor_tensor(
                out=result[:],
                in0=acc[group][:, 1, :],
                scalar=chooser[group][1][:],
                in1=part[group][:],
                op0=MULT,
                op1=ADD,
            )
            first, w, start = GROUPS[group][1][0]
            nc.sync.dma_start(out=out_rows[:, first : first + w, :], in_=result[:])

        PASS_LAG = 5
        FIRST_LAG = 5
        SECOND_LAG = 6
        complete = {}
        for step, (group, side) in enumerate(pieces):
            complete[group] = step
        n = len(pieces)
        for step in range(n + 3):
            if step < n:
                turn(*pieces[step])
            if 1 <= step < n + 1:
                quantise(*pieces[step - 1])
            for group in range(LAST):
                if step == complete[group] + PASS_LAG:
                    multiply(group)
                if step == complete[group] + FIRST_LAG:
                    choose_first(group)
                if step == complete[group] + SECOND_LAG:
                    choose_second(group)

        for side in range(2):
            last_acc = one_pass(LAST, 2 * LAST + side - 1)
            last_result = keep.tile([P, FI], F32, name="last_result_%d" % side)
            if side == 0:
                nc.scalar.copy(out=last_result[:], in_=last_acc[:, 1, :])
                runs = GROUPS[LAST][1][:3]
            else:
                nc.vector.tensor_copy(out=last_result[:], in_=last_acc[:, 1, :])
                runs = GROUPS[LAST][1][3:]
            for first, w, start in runs:
                nc.sync.dma_start(out=out_rows[:, first : first + w, :], in_=last_result[start : P : RUN // w, :])
